import numpy as np
import ml_dtypes

BF16 = ml_dtypes.bfloat16


def bf(x):
    return np.asarray(x, np.float32).astype(BF16)


def f32(x):
    return np.asarray(x, np.float32)


def f64(x):
    return np.asarray(x).astype(np.float64)


def striped(idx):
    return np.tile(idx.reshape(-1, 16).T, (8, 1))


D, E, M, S, K, H, N = 128, 128, 128, 1024, 8, 512, 8192


def setup_inputs():
    return {"x": bf(np.random.standard_normal((D, S))), "wc": bf(np.random.standard_normal((D, M)) / np.sqrt(D)), "wn": bf(np.random.standard_normal((D, M)) * np.sqrt(K / D)), "we": bf(np.random.standard_normal((E, M)) * np.sqrt(K / E)), "e": f32(np.random.standard_normal((E, N))), "offs": striped(np.concatenate([np.random.permutation(S)[:H] for _ in range(N // H)]))}


def reference(x, wc, wn, we, e, offs):
    idx = offs[:16].T.reshape(-1)
    xs = f64(x)
    nb = xs[:, idx].reshape(D, K, S).mean(axis=1)
    eb = f64(e).reshape(E, K, S).mean(axis=1)
    return np.maximum(f64(wc).T @ xs + f64(wn).T @ nb + f64(we).T @ eb, 0.0)

@@ -1,0 +1,80 @@
+import concourse.mybir as mybir
+
+BF16, F32, U16 = mybir.dt.bfloat16, mybir.dt.float32, mybir.dt.uint16
+ADD = mybir.AluOpType.add
+RELU = mybir.ActivationFunctionType.Relu
+
+P = 128
+NODES = 1024
+DEGREE = 8
+BANK = 512
+HALVES = NODES // BANK
+LIST = DEGREE * NODES
+
+FLOPS = 2 * P * P * (NODES + LIST + NODES)
+
+
+def tile_gcnn_kernel(tc, x, wc, wn, we, e, offs, out):
+    nc = tc.nc
+    with (
+        tc.tile_pool(name="held", bufs=1) as held,
+        tc.psum_pool(name="psum", bufs=1) as psum,
+    ):
+        offsets = held.tile([P, LIST // 16], U16, name="offsets")
+        nc.sync.dma_start(offsets[:], offs)
+        nodes = held.tile([P, NODES], BF16, name="nodes")
+        nc.scalar.dma_start(nodes[:], x)
+        wn_raw = held.tile([P, P], BF16, name="wn_raw")
+        nc.gpsimd.dma_start(wn_raw[:], wn)
+        wc_own = held.tile([P, P], BF16, name="wc_own")
+        nc.gpsimd.dma_start(wc_own[:], wc)
+        we_raw = held.tile([P, P], BF16, name="we_raw")
+        nc.gpsimd.dma_start(we_raw[:], we)
+
+        edges = []
+        for k in range(DEGREE):
+            block = held.tile([P, NODES], F32, name=f"edges{k}")
+            queue = nc.sync if k % 2 == 0 else nc.scalar
+            queue.dma_start(block[:], e[:, k * NODES : (k + 1) * NODES])
+            edges.append(block)
+
+        wn_mean = held.tile([P, P], BF16, name="wn_mean")
+        nc.vector.tensor_scalar_mul(wn_mean[:], wn_raw[:], 1.0 / DEGREE)
+        we_mean = held.tile([P, P], BF16, name="we_mean")
+        nc.scalar.mul(we_mean[:], we_raw[:], 1.0 / DEGREE)
+
+        banks = [psum.tile([P, BANK], F32, name=f"bank{h}") for h in range(HALVES)]
+        for h in range(HALVES):
+            nc.tensor.matmul(
+                banks[h][:], wc_own[:], nodes[:, h * BANK : (h + 1) * BANK], start=True, stop=False
+            )
+        for h in range(HALVES):
+            for k in range(DEGREE):
+                first = (k * NODES + h * BANK) // 16
+                neighbours = nodes[:].indirect(offsets[:, first : first + BANK // 16])
+                nc.tensor.matmul(banks[h][:], wn_mean[:], neighbours, start=False, stop=False)
+
+        edge_sums = []
+        for h in range(HALVES):
+            cols = slice(h * BANK, (h + 1) * BANK)
+            running = held.tile([P, BANK], F32, name=f"running{h}")
+            nc.vector.tensor_tensor(running[:], edges[0][:, cols], edges[1][:, cols], ADD)
+            edge_sums.append(running)
+        for k in range(2, DEGREE - 1):
+            for h in range(HALVES):
+                cols = slice(h * BANK, (h + 1) * BANK)
+                nc.vector.tensor_tensor(edge_sums[h][:], edge_sums[h][:], edges[k][:, cols], ADD)
+
+        for h in range(HALVES):
+            cols = slice(h * BANK, (h + 1) * BANK)
+            rounded = held.tile([P, BANK], BF16, name=f"rounded{h}")
+            nc.vector.tensor_tensor(rounded[:], edge_sums[h][:], edges[DEGREE - 1][:, cols], ADD)
+            nc.tensor.matmul(banks[h][:], we_mean[:], rounded[:], start=False, stop=True)
+
+            result = held.tile([P, BANK], F32, name=f"result{h}")
+            if h == 0:
+                nc.scalar.activation(result[:], banks[h][:], RELU)
+                nc.scalar.dma_start(out[:, cols], result[:])
+            else:
+                nc.vector.tensor_scalar_max(result[:], banks[h][:], 0.0)
+                nc.sync.dma_start(out[:, cols], result[:])

@@ -20,16 +20,16 @@ def tile_gcnn_kernel(tc, x, wc, wn, we, e, offs, out):
         tc.tile_pool(name="held", bufs=1) as held,
         tc.psum_pool(name="psum", bufs=1) as psum,
     ):
+        wn_raw = held.tile([P, P], BF16, name="wn_raw")
+        nc.sync.dma_start(wn_raw[:], wn)
         offsets = held.tile([P, LIST // 16], U16, name="offsets")
         nc.sync.dma_start(offsets[:], offs)
         nodes = held.tile([P, NODES], BF16, name="nodes")
         nc.scalar.dma_start(nodes[:], x)
-        wn_raw = held.tile([P, P], BF16, name="wn_raw")
-        nc.gpsimd.dma_start(wn_raw[:], wn)
         wc_own = held.tile([P, P], BF16, name="wc_own")
-        nc.gpsimd.dma_start(wc_own[:], wc)
+        nc.scalar.dma_start(wc_own[:], wc)
         we_raw = held.tile([P, P], BF16, name="we_raw")
-        nc.gpsimd.dma_start(we_raw[:], we)
+        nc.scalar.dma_start(we_raw[:], we)
 
         edges = []
         for k in range(DEGREE):

@@ -10,6 +10,7 @@ DEGREE = 8
 BANK = 512
 HALVES = NODES // BANK
 LIST = DEGREE * NODES
+WARM_UP = 8
 
 FLOPS = 2 * P * P * (NODES + LIST + NODES)
 
@@ -37,6 +38,12 @@ def tile_gcnn_kernel(tc, x, wc, wn, we, e, offs, out):
             queue = nc.sync if k % 2 == 0 else nc.scalar
             queue.dma_start(block[:], e[:, k * NODES : (k + 1) * NODES])
             edges.append(block)
+
+        zeros = held.tile([P, BANK], BF16, name="zeros")
+        nc.vector.memset(zeros[:], 0.0)
+        unread = psum.tile([P, BANK], F32, name="unread")
+        for i in range(WARM_UP):
+            nc.tensor.matmul(unread[:], zeros[:, :P], zeros[:], start=True, stop=True)
 
         wn_mean = held.tile([P, P], BF16, name="wn_mean")
         nc.vector.tensor_scalar_mul(wn_mean[:], wn_raw[:], 1.0 / DEGREE)

@@ -10,7 +10,6 @@ DEGREE = 8
 BANK = 512
 HALVES = NODES // BANK
 LIST = DEGREE * NODES
-WARM_UP = 8
 
 FLOPS = 2 * P * P * (NODES + LIST + NODES)
 
@@ -39,12 +38,6 @@ def tile_gcnn_kernel(tc, x, wc, wn, we, e, offs, out):
             queue.dma_start(block[:], e[:, k * NODES : (k + 1) * NODES])
             edges.append(block)
 
-        zeros = held.tile([P, BANK], BF16, name="zeros")
-        nc.vector.memset(zeros[:], 0.0)
-        unread = psum.tile([P, BANK], F32, name="unread")
-        for i in range(WARM_UP):
-            nc.tensor.matmul(unread[:], zeros[:, :P], zeros[:], start=True, stop=True)
-
         wn_mean = held.tile([P, P], BF16, name="wn_mean")
         nc.vector.tensor_scalar_mul(wn_mean[:], wn_raw[:], 1.0 / DEGREE)
         we_mean = held.tile([P, P], BF16, name="we_mean")
@@ -61,21 +54,15 @@ def tile_gcnn_kernel(tc, x, wc, wn, we, e, offs, out):
                 neighbours = nodes[:].indirect(offsets[:, first : first + BANK // 16])
                 nc.tensor.matmul(banks[h][:], wn_mean[:], neighbours, start=False, stop=False)
 
-        edge_sums = []
-        for h in range(HALVES):
-            cols = slice(h * BANK, (h + 1) * BANK)
-            running = held.tile([P, BANK], F32, name=f"running{h}")
-            nc.vector.tensor_tensor(running[:], edges[0][:, cols], edges[1][:, cols], ADD)
-            edge_sums.append(running)
+        running = held.tile([P, NODES], F32, name="running")
+        nc.vector.tensor_tensor(running[:], edges[0][:], edges[1][:], ADD)
         for k in range(2, DEGREE - 1):
-            for h in range(HALVES):
-                cols = slice(h * BANK, (h + 1) * BANK)
-                nc.vector.tensor_tensor(edge_sums[h][:], edge_sums[h][:], edges[k][:, cols], ADD)
+            nc.vector.tensor_tensor(running[:], running[:], edges[k][:], ADD)
 
         for h in range(HALVES):
             cols = slice(h * BANK, (h + 1) * BANK)
             rounded = held.tile([P, BANK], BF16, name=f"rounded{h}")
-            nc.vector.tensor_tensor(rounded[:], edge_sums[h][:], edges[DEGREE - 1][:, cols], ADD)
+            nc.vector.tensor_tensor(rounded[:], running[:, cols], edges[DEGREE - 1][:, cols], ADD)
             nc.tensor.matmul(banks[h][:], we_mean[:], rounded[:], start=False, stop=True)
 
             result = held.tile([P, BANK], F32, name=f"result{h}")

@@ -20,23 +20,28 @@ def tile_gcnn_kernel(tc, x, wc, wn, we, e, offs, out):
         tc.tile_pool(name="held", bufs=1) as held,
         tc.psum_pool(name="psum", bufs=1) as psum,
     ):
+        nodes = held.tile([P, NODES], BF16, name="nodes")
+        nc.scalar.dma_start(nodes[:], x)
         wn_raw = held.tile([P, P], BF16, name="wn_raw")
         nc.sync.dma_start(wn_raw[:], wn)
         offsets = held.tile([P, LIST // 16], U16, name="offsets")
         nc.sync.dma_start(offsets[:], offs)
-        nodes = held.tile([P, NODES], BF16, name="nodes")
-        nc.scalar.dma_start(nodes[:], x)
         wc_own = held.tile([P, P], BF16, name="wc_own")
-        nc.scalar.dma_start(wc_own[:], wc)
+        nc.sync.dma_start(wc_own[:], wc)
         we_raw = held.tile([P, P], BF16, name="we_raw")
-        nc.scalar.dma_start(we_raw[:], we)
+        nc.sync.dma_start(we_raw[:], we)
 
         edges = []
-        for k in range(DEGREE):
+        for k in range(DEGREE - 1):
             block = held.tile([P, NODES], F32, name=f"edges{k}")
-            queue = nc.sync if k % 2 == 0 else nc.scalar
-            queue.dma_start(block[:], e[:, k * NODES : (k + 1) * NODES])
+            nc.sync.dma_start(block[:], e[:, k * NODES : (k + 1) * NODES])
             edges.append(block)
+        last_edges = []
+        for h in range(HALVES):
+            first = (DEGREE - 1) * NODES + h * BANK
+            half_block = held.tile([P, BANK], F32, name=f"last_edges{h}")
+            nc.sync.dma_start(half_block[:], e[:, first : first + BANK])
+            last_edges.append(half_block)
 
         wn_mean = held.tile([P, P], BF16, name="wn_mean")
         nc.vector.tensor_scalar_mul(wn_mean[:], wn_raw[:], 1.0 / DEGREE)
@@ -54,15 +59,21 @@ def tile_gcnn_kernel(tc, x, wc, wn, we, e, offs, out):
                 neighbours = nodes[:].indirect(offsets[:, first : first + BANK // 16])
                 nc.tensor.matmul(banks[h][:], wn_mean[:], neighbours, start=False, stop=False)
 
-        running = held.tile([P, NODES], F32, name="running")
-        nc.vector.tensor_tensor(running[:], edges[0][:], edges[1][:], ADD)
+        edge_sums = []
+        for h in range(HALVES):
+            cols = slice(h * BANK, (h + 1) * BANK)
+            running = held.tile([P, BANK], F32, name=f"running{h}")
+            nc.vector.tensor_tensor(running[:], edges[0][:, cols], edges[1][:, cols], ADD)
+            edge_sums.append(running)
         for k in range(2, DEGREE - 1):
-            nc.vector.tensor_tensor(running[:], running[:], edges[k][:], ADD)
+            for h in range(HALVES):
+                cols = slice(h * BANK, (h + 1) * BANK)
+                nc.vector.tensor_tensor(edge_sums[h][:], edge_sums[h][:], edges[k][:, cols], ADD)
 
         for h in range(HALVES):
             cols = slice(h * BANK, (h + 1) * BANK)
             rounded = held.tile([P, BANK], BF16, name=f"rounded{h}")
-            nc.vector.tensor_tensor(rounded[:], running[:, cols], edges[DEGREE - 1][:, cols], ADD)
+            nc.vector.tensor_tensor(rounded[:], edge_sums[h][:], last_edges[h][:], ADD)
             nc.tensor.matmul(banks[h][:], we_mean[:], rounded[:], start=False, stop=True)
 
             result = held.tile([P, BANK], F32, name=f"result{h}")

@@ -21,15 +21,15 @@ def tile_gcnn_kernel(tc, x, wc, wn, we, e, offs, out):
         tc.psum_pool(name="psum", bufs=1) as psum,
     ):
         nodes = held.tile([P, NODES], BF16, name="nodes")
-        nc.scalar.dma_start(nodes[:], x)
-        wn_raw = held.tile([P, P], BF16, name="wn_raw")
-        nc.sync.dma_start(wn_raw[:], wn)
+        nc.sync.dma_start(nodes[:], x)
         offsets = held.tile([P, LIST // 16], U16, name="offsets")
         nc.sync.dma_start(offsets[:], offs)
         wc_own = held.tile([P, P], BF16, name="wc_own")
-        nc.sync.dma_start(wc_own[:], wc)
+        nc.scalar.dma_start(wc_own[:], wc)
+        wn_raw = held.tile([P, P], BF16, name="wn_raw")
+        nc.scalar.dma_start(wn_raw[:], wn)
         we_raw = held.tile([P, P], BF16, name="we_raw")
-        nc.sync.dma_start(we_raw[:], we)
+        nc.scalar.dma_start(we_raw[:], we)
 
         edges = []
         for k in range(DEGREE - 1):

@@ -10,6 +10,7 @@ DEGREE = 8
 BANK = 512
 HALVES = NODES // BANK
 LIST = DEGREE * NODES
+SPLIT_FROM = DEGREE - 2
 
 FLOPS = 2 * P * P * (NODES + LIST + NODES)
 
@@ -31,17 +32,16 @@ def tile_gcnn_kernel(tc, x, wc, wn, we, e, offs, out):
         we_raw = held.tile([P, P], BF16, name="we_raw")
         nc.scalar.dma_start(we_raw[:], we)
 
-        edges = []
-        for k in range(DEGREE - 1):
+        first_two = held.tile([P, 2 * NODES], F32, name="first_two")
+        nc.sync.dma_start(first_two[:], e[:, : 2 * NODES])
+        edges = [first_two[:, :NODES], first_two[:, NODES:]]
+        for k in range(2, DEGREE):
             block = held.tile([P, NODES], F32, name=f"edges{k}")
-            nc.sync.dma_start(block[:], e[:, k * NODES : (k + 1) * NODES])
-            edges.append(block)
-        last_edges = []
-        for h in range(HALVES):
-            first = (DEGREE - 1) * NODES + h * BANK
-            half_block = held.tile([P, BANK], F32, name=f"last_edges{h}")
-            nc.sync.dma_start(half_block[:], e[:, first : first + BANK])
-            last_edges.append(half_block)
+            width = BANK if k >= SPLIT_FROM else NODES
+            for first in range(0, NODES, width):
+                column = k * NODES + first
+                nc.sync.dma_start(block[:, first : first + width], e[:, column : column + width])
+            edges.append(block[:])
 
         wn_mean = held.tile([P, P], BF16, name="wn_mean")
         nc.vector.tensor_scalar_mul(wn_mean[:], wn_raw[:], 1.0 / DEGREE)
@@ -73,7 +73,7 @@ def tile_gcnn_kernel(tc, x, wc, wn, we, e, offs, out):
         for h in range(HALVES):
             cols = slice(h * BANK, (h + 1) * BANK)
             rounded = held.tile([P, BANK], BF16, name=f"rounded{h}")
-            nc.vector.tensor_tensor(rounded[:], edge_sums[h][:], last_edges[h][:], ADD)
+            nc.vector.tensor_tensor(rounded[:], edge_sums[h][:], edges[DEGREE - 1][:, cols], ADD)
             nc.tensor.matmul(banks[h][:], we_mean[:], rounded[:], start=False, stop=True)
 
             result = held.tile([P, BANK], F32, name=f"result{h}")

@@ -10,7 +10,7 @@ DEGREE = 8
 BANK = 512
 HALVES = NODES // BANK
 LIST = DEGREE * NODES
-SPLIT_FROM = DEGREE - 2
+PIECE = BANK // 2
 
 FLOPS = 2 * P * P * (NODES + LIST + NODES)
 
@@ -35,13 +35,15 @@ def tile_gcnn_kernel(tc, x, wc, wn, we, e, offs, out):
         first_two = held.tile([P, 2 * NODES], F32, name="first_two")
         nc.sync.dma_start(first_two[:], e[:, : 2 * NODES])
         edges = [first_two[:, :NODES], first_two[:, NODES:]]
-        for k in range(2, DEGREE):
+        for k in range(2, DEGREE - 2):
             block = held.tile([P, NODES], F32, name=f"edges{k}")
-            width = BANK if k >= SPLIT_FROM else NODES
-            for first in range(0, NODES, width):
-                column = k * NODES + first
-                nc.sync.dma_start(block[:, first : first + width], e[:, column : column + width])
+            nc.sync.dma_start(block[:], e[:, k * NODES : (k + 1) * NODES])
             edges.append(block[:])
+        by_edge = e.rearrange("p (k n) -> p k n", k=DEGREE)
+        last_two = [held.tile([P, 2, BANK], F32, name=f"last_two{h}") for h in range(HALVES)]
+        nc.sync.dma_start(last_two[0][:], by_edge[:, DEGREE - 2 :, :BANK])
+        for i in range(2):
+            nc.sync.dma_start(last_two[1][:, i], by_edge[:, DEGREE - 2 + i, BANK:])
 
         wn_mean = held.tile([P, P], BF16, name="wn_mean")
         nc.vector.tensor_scalar_mul(wn_mean[:], wn_raw[:], 1.0 / DEGREE)
@@ -65,21 +67,29 @@ def tile_gcnn_kernel(tc, x, wc, wn, we, e, offs, out):
             running = held.tile([P, BANK], F32, name=f"running{h}")
             nc.vector.tensor_tensor(running[:], edges[0][:, cols], edges[1][:, cols], ADD)
             edge_sums.append(running)
-        for k in range(2, DEGREE - 1):
+        for k in range(2, DEGREE - 2):
             for h in range(HALVES):
                 cols = slice(h * BANK, (h + 1) * BANK)
                 nc.vector.tensor_tensor(edge_sums[h][:], edge_sums[h][:], edges[k][:, cols], ADD)
-
+        rounded = [held.tile([P, BANK], BF16, name=f"rounded{h}") for h in range(HALVES)]
+        results = [held.tile([P, BANK], F32, name=f"result{h}") for h in range(HALVES)]
         for h in range(HALVES):
-            cols = slice(h * BANK, (h + 1) * BANK)
-            rounded = held.tile([P, BANK], BF16, name=f"rounded{h}")
-            nc.vector.tensor_tensor(rounded[:], edge_sums[h][:], edges[DEGREE - 1][:, cols], ADD)
-            nc.tensor.matmul(banks[h][:], we_mean[:], rounded[:], start=False, stop=True)
-
-            result = held.tile([P, BANK], F32, name=f"result{h}")
-            if h == 0:
-                nc.scalar.activation(result[:], banks[h][:], RELU)
-                nc.scalar.dma_start(out[:, cols], result[:])
-            else:
-                nc.vector.tensor_scalar_max(result[:], banks[h][:], 0.0)
-                nc.sync.dma_start(out[:, cols], result[:])
+            nc.vector.tensor_tensor(edge_sums[h][:], edge_sums[h][:], last_two[h][:, 0], ADD)
+            width = BANK if h == 0 else PIECE
+            pieces = [slice(first, first + width) for first in range(0, BANK, width)]
+            for cols in pieces:
+                nc.vector.tensor_tensor(
+                    rounded[h][:, cols], edge_sums[h][:, cols], last_two[h][:, 1, cols], ADD
+                )
+                closes = cols.stop == BANK
+                nc.tensor.matmul(
+                    banks[h][:, cols], we_mean[:], rounded[h][:, cols], start=False, stop=closes
+                )
+            for cols in pieces:
+                target = out[:, h * BANK + cols.start : h * BANK + cols.stop]
+                if h == 0:
+                    nc.scalar.activation(results[h][:, cols], banks[h][:, cols], RELU)
+                    nc.scalar.dma_start(target, results[h][:, cols])
+                else:
+                    nc.vector.tensor_scalar_max(results[h][:, cols], banks[h][:, cols], 0.0)
+                    nc.sync.dma_start(target, results[h][:, cols])

@@ -73,14 +73,17 @@ def tile_gcnn_kernel(tc, x, wc, wn, we, e, offs, out):
                 nc.vector.tensor_tensor(edge_sums[h][:], edge_sums[h][:], edges[k][:, cols], ADD)
         rounded = [held.tile([P, BANK], BF16, name=f"rounded{h}") for h in range(HALVES)]
         results = [held.tile([P, BANK], F32, name=f"result{h}") for h in range(HALVES)]
+        quarters = [slice(first, first + PIECE) for first in range(0, BANK, PIECE)]
         for h in range(HALVES):
-            nc.vector.tensor_tensor(edge_sums[h][:], edge_sums[h][:], last_two[h][:, 0], ADD)
-            width = BANK if h == 0 else PIECE
-            pieces = [slice(first, first + width) for first in range(0, BANK, width)]
-            for cols in pieces:
+            sums = edge_sums[h]
+            for cols in quarters:
+                nc.vector.tensor_tensor(sums[:, cols], sums[:, cols], last_two[h][:, 0, cols], ADD)
+            for cols in quarters:
                 nc.vector.tensor_tensor(
-                    rounded[h][:, cols], edge_sums[h][:, cols], last_two[h][:, 1, cols], ADD
+                    rounded[h][:, cols], sums[:, cols], last_two[h][:, 1, cols], ADD
                 )
+            pieces = [slice(0, BANK)] if h == 0 else quarters
+            for cols in pieces:
                 closes = cols.stop == BANK
                 nc.tensor.matmul(
                     banks[h][:, cols], we_mean[:], rounded[h][:, cols], start=False, stop=closes

@@ -29,8 +29,6 @@ def tile_gcnn_kernel(tc, x, wc, wn, we, e, offs, out):
         nc.scalar.dma_start(wc_own[:], wc)
         wn_raw = held.tile([P, P], BF16, name="wn_raw")
         nc.scalar.dma_start(wn_raw[:], wn)
-        we_raw = held.tile([P, P], BF16, name="we_raw")
-        nc.scalar.dma_start(we_raw[:], we)
 
         first_two = held.tile([P, 2 * NODES], F32, name="first_two")
         nc.sync.dma_start(first_two[:], e[:, : 2 * NODES])
@@ -42,6 +40,8 @@ def tile_gcnn_kernel(tc, x, wc, wn, we, e, offs, out):
         by_edge = e.rearrange("p (k n) -> p k n", k=DEGREE)
         last_two = [held.tile([P, 2, BANK], F32, name=f"last_two{h}") for h in range(HALVES)]
         nc.sync.dma_start(last_two[0][:], by_edge[:, DEGREE - 2 :, :BANK])
+        we_raw = held.tile([P, P], BF16, name="we_raw")
+        nc.sync.dma_start(we_raw[:], we)
         for i in range(2):
             nc.sync.dma_start(last_two[1][:, i], by_edge[:, DEGREE - 2 + i, BANK:])
 

import concourse.mybir as mybir

BF16, F32, U16 = mybir.dt.bfloat16, mybir.dt.float32, mybir.dt.uint16
ADD = mybir.AluOpType.add
RELU = mybir.ActivationFunctionType.Relu

P = 128
NODES = 1024
DEGREE = 8
BANK = 512
HALVES = NODES // BANK
LIST = DEGREE * NODES
PIECE = BANK // 2

FLOPS = 2 * P * P * (NODES + LIST + NODES)


def tile_gcnn_kernel(tc, x, wc, wn, we, e, offs, out):
    nc = tc.nc
    with (
        tc.tile_pool(name="held", bufs=1) as held,
        tc.psum_pool(name="psum", bufs=1) as psum,
    ):
        nodes = held.tile([P, NODES], BF16, name="nodes")
        nc.sync.dma_start(nodes[:], x)
        offsets = held.tile([P, LIST // 16], U16, name="offsets")
        nc.sync.dma_start(offsets[:], offs)
        wc_own = held.tile([P, P], BF16, name="wc_own")
        nc.scalar.dma_start(wc_own[:], wc)
        wn_raw = held.tile([P, P], BF16, name="wn_raw")
        nc.scalar.dma_start(wn_raw[:], wn)

        first_two = held.tile([P, 2 * NODES], F32, name="first_two")
        nc.sync.dma_start(first_two[:], e[:, : 2 * NODES])
        edges = [first_two[:, :NODES], first_two[:, NODES:]]
        for k in range(2, DEGREE - 2):
            block = held.tile([P, NODES], F32, name=f"edges{k}")
            nc.sync.dma_start(block[:], e[:, k * NODES : (k + 1) * NODES])
            edges.append(block[:])
        by_edge = e.rearrange("p (k n) -> p k n", k=DEGREE)
        last_two = [held.tile([P, 2, BANK], F32, name=f"last_two{h}") for h in range(HALVES)]
        nc.sync.dma_start(last_two[0][:], by_edge[:, DEGREE - 2 :, :BANK])
        we_raw = held.tile([P, P], BF16, name="we_raw")
        nc.sync.dma_start(we_raw[:], we)
        for i in range(2):
            nc.sync.dma_start(last_two[1][:, i], by_edge[:, DEGREE - 2 + i, BANK:])

        wn_mean = held.tile([P, P], BF16, name="wn_mean")
        nc.vector.tensor_scalar_mul(wn_mean[:], wn_raw[:], 1.0 / DEGREE)
        we_mean = held.tile([P, P], BF16, name="we_mean")
        nc.scalar.mul(we_mean[:], we_raw[:], 1.0 / DEGREE)

        banks = [psum.tile([P, BANK], F32, name=f"bank{h}") for h in range(HALVES)]
        for h in range(HALVES):
            nc.tensor.matmul(
                banks[h][:], wc_own[:], nodes[:, h * BANK : (h + 1) * BANK], start=True, stop=False
            )
        for h in range(HALVES):
            for k in range(DEGREE):
                first = (k * NODES + h * BANK) // 16
                neighbours = nodes[:].indirect(offsets[:, first : first + BANK // 16])
                nc.tensor.matmul(banks[h][:], wn_mean[:], neighbours, start=False, stop=False)

        edge_sums = []
        for h in range(HALVES):
            cols = slice(h * BANK, (h + 1) * BANK)
            running = held.tile([P, BANK], F32, name=f"running{h}")
            nc.vector.tensor_tensor(running[:], edges[0][:, cols], edges[1][:, cols], ADD)
            edge_sums.append(running)
        for k in range(2, DEGREE - 2):
            for h in range(HALVES):
                cols = slice(h * BANK, (h + 1) * BANK)
                nc.vector.tensor_tensor(edge_sums[h][:], edge_sums[h][:], edges[k][:, cols], ADD)
        rounded = [held.tile([P, BANK], BF16, name=f"rounded{h}") for h in range(HALVES)]
        results = [held.tile([P, BANK], F32, name=f"result{h}") for h in range(HALVES)]
        quarters = [slice(first, first + PIECE) for first in range(0, BANK, PIECE)]
        for h in range(HALVES):
            sums = edge_sums[h]
            for cols in quarters:
                nc.vector.tensor_tensor(sums[:, cols], sums[:, cols], last_two[h][:, 0, cols], ADD)
            for cols in quarters:
                nc.vector.tensor_tensor(
                    rounded[h][:, cols], sums[:, cols], last_two[h][:, 1, cols], ADD
                )
            pieces = [slice(0, BANK)] if h == 0 else quarters
            for cols in pieces:
                closes = cols.stop == BANK
                nc.tensor.matmul(
                    banks[h][:, cols], we_mean[:], rounded[h][:, cols], start=False, stop=closes
                )
            for cols in pieces:
                target = out[:, h * BANK + cols.start : h * BANK + cols.stop]
                if h == 0:
                    nc.scalar.activation(results[h][:, cols], banks[h][:, cols], RELU)
                    nc.scalar.dma_start(target, results[h][:, cols])
                else:
                    nc.vector.tensor_scalar_max(results[h][:, cols], banks[h][:, cols], 0.0)
                    nc.sync.dma_start(target, results[h][:, cols])
